import numpy as np
import ml_dtypes


def mxq(x, axis, fmt="e4m3"):
    dtype, down = {"e4m3": (ml_dtypes.float8_e4m3fn, 7), "e5m2": (ml_dtypes.float8_e5m2, 14)}[fmt]
    v = np.moveaxis(np.asarray(x, np.float32).astype(ml_dtypes.bfloat16).astype(np.float64), axis, -1)
    blocks = v.reshape(v.shape[:-1] + (-1, 32))
    amax = np.abs(blocks).max(-1, keepdims=True)
    byte = np.maximum(np.where(amax > 0, np.frexp(amax)[1] - 1 + 127, 0) - down, 1)
    scale = np.exp2(byte - 127.0)
    codes = (blocks / scale).astype(np.float32).astype(dtype).astype(np.float64)
    return np.moveaxis((codes * scale).reshape(v.shape), -1, axis)


WIDE = False


def mx_kscale(k):
    if not WIDE:
        return np.ones(k)
    levels = np.array([10, -10, 5, -5, 0])
    if k % 512:
        return np.exp2(np.random.permutation(np.resize(levels, k // 32))).repeat(32)
    a = np.empty((k // 512, 16))
    for p in range(k // 512):
        a[p, :8] = np.random.permutation(np.resize(levels, 8))
        for g in range(8):
            far = levels[np.abs(levels - a[p, g]) >= 10]
            a[p, g + 8] = far[np.random.randint(len(far))]
    return np.exp2(a.ravel()).repeat(32)


BF16 = ml_dtypes.bfloat16


def bf(x):
    return np.asarray(x, np.float32).astype(BF16)


def f64(x):
    return np.asarray(x).astype(np.float64)


E2M1 = np.array([0.0, 0.5, 1.0, 1.5, 2.0, 3.0, 4.0, 6.0, -0.0, -0.5, -1.0, -1.5, -2.0, -3.0, -4.0, -6.0])


def pack_weight(w, fmt):
    k, n = w.shape
    w = f64(bf(w)).reshape(k // 32, 32, n)
    amax = np.abs(w).max(1)
    if fmt == "e4m3":
        byte = np.frexp(amax)[1] - 1 + 127 - 7
    else:
        mant, ex = np.frexp(amax / 6.0)
        byte = np.where(mant > 0.5, ex, ex - 1) + 127
    byte = np.clip(np.where(amax > 0, byte, 1), 1, 254)
    scaled = (w * np.exp2(127.0 - byte)[:, None, :]).reshape(k, n).astype(np.float32)
    by_word = np.ascontiguousarray(scaled.reshape(k // 512, 128, 4, n).transpose(0, 1, 3, 2))
    if fmt == "e4m3":
        words = by_word.astype(ml_dtypes.float8_e4m3fn).view(np.uint8)
    else:
        c = by_word.astype(ml_dtypes.float4_e2m1fn).view(np.uint8) & 0xF
        words = c[..., 0::2] | (c[..., 1::2] << 4)
    return np.ascontiguousarray(words), np.ascontiguousarray(byte.astype(np.uint8).reshape(k // 512, 16, n))


def unpack_weight(words, scales, fmt):
    g, p, n, _ = words.shape
    if fmt == "e4m3":
        vals = np.ascontiguousarray(words).view(ml_dtypes.float8_e4m3fn).astype(np.float64)
    else:
        nib = np.empty((g, p, n, 4), np.uint8)
        nib[..., 0::2] = words & 0xF
        nib[..., 1::2] = words >> 4
        vals = E2M1[nib]
    vals = vals * np.repeat(np.exp2(scales.astype(np.float64) - 127.0), 8, axis=1)[..., None]
    return vals.transpose(0, 1, 3, 2).reshape(g * 512, n)


B, C, CI, N = 2, 1024, 512, 1024
EPS = 1e-5


def setup_inputs():
    s, t = mx_kscale(N), mx_kscale(CI)
    r = np.random.standard_normal
    affinity = bf(r((B, N, N)) * 0.2 * s[None, None, :])
    g_x = bf(r((B, N, CI)) / s[None, :, None] * t[None, None, :])
    w = r((C, CI)) * 1.5 / (0.2 * np.sqrt(N) * np.sqrt(CI)) / t[None, :]
    w_w_words, w_w_scales = pack_weight(np.ascontiguousarray(w.T), "e4m3")
    return {"affinity": affinity,
            "g_x": g_x,
            "w_w_words": w_w_words,
            "w_w_scales": w_w_scales,
            "w_b": bf(r(C) * 0.3),
            "bn_gamma": bf(r(C)),
            "bn_beta": bf(r(C) * 0.5),
            "bn_mean": bf(r(C) * 0.5),
            "bn_var": bf(np.random.uniform(0.5, 1.5, C)),
            "x": bf(r((B, C, N)))}


def reference(affinity, g_x, w_w_words, w_w_scales, w_b, bn_gamma, bn_beta, bn_mean, bn_var, x):
    y = (mxq(f64(affinity), 2, "e4m3") @ mxq(f64(g_x), 1, "e4m3")).transpose(0, 2, 1)
    wy = (unpack_weight(w_w_words, w_w_scales, "e4m3").T @ mxq(y, 1, "e4m3")) + f64(w_b)[None, :, None]
    inv_std = 1.0 / np.sqrt(f64(bn_var) + EPS)
    wy = f64(bn_gamma)[None, :, None] * (wy - f64(bn_mean)[None, :, None]) * inv_std[None, :, None] + f64(bn_beta)[None, :, None]
    return wy + f64(x)

@@ -1,0 +1,258 @@
+from contextlib import ExitStack
+
+import concourse.mybir as mybir
+from concourse.masks import make_identity
+
+F32 = mybir.dt.float32
+BF16 = mybir.dt.bfloat16
+I32 = mybir.dt.int32
+U32 = mybir.dt.uint32
+U8 = mybir.dt.uint8
+FP8X4 = mybir.dt.float8_e4m3fn_x4
+ALU = mybir.AluOpType
+ACT = mybir.ActivationFunctionType
+
+P = 128
+LANES = 4
+K_PASS = P * LANES
+BANK = 512
+
+BATCH = 2
+POINTS = 1024
+INNER = 512
+CHANNELS = 1024
+EPS = 1e-5
+
+PASSES = POINTS // K_PASS
+QBLOCK = 2 * P
+QUARTERS = POINTS // QBLOCK
+BLOCKS = BATCH * QUARTERS
+HALVES = POINTS // BANK
+CTILES = CHANNELS // P
+
+TURN_AHEAD = 1
+REGROUP_AHEAD = 2
+QUANTISE_AHEAD = 1
+PROJECT_LAG = QUARTERS
+SHIFT_LAG = PROJECT_LAG - 1
+GAIN_STEP = SHIFT_LAG - 2
+
+FLOPS = 2 * BATCH * (POINTS * POINTS * INNER + CHANNELS * INNER * POINTS)
+
+
+def tile_sgcam_pb_kernel(
+    tc, affinity, g_x, w_w_words, w_w_scales, w_b, bn_gamma, bn_beta, bn_mean, bn_var, x, out
+):
+    nc = tc.nc
+    with ExitStack() as ctx:
+        keep = ctx.enter_context(tc.tile_pool(name="keep", bufs=1))
+        stage = ctx.enter_context(tc.tile_pool(name="stage", bufs=3))
+        psum = ctx.enter_context(tc.psum_pool(name="psum", bufs=8))
+
+        identity = keep.tile([P, P], F32, name="identity")
+        make_identity(nc, identity[:])
+        minus_half = keep.tile([P, CTILES], F32, name="minus_half")
+        nc.gpsimd.memset(minus_half[:], -0.5)
+        w_scales = keep.tile([P, CHANNELS], U8, name="w_scales", align_bytes=64)
+        nc.vector.memset(w_scales[:].bitcast(I32), 0)
+        vector_rows = keep.tile([P, P], BF16, name="vector_rows")
+        nc.vector.memset(vector_rows[:], 0.0)
+        warm = keep.tile([P, 1], F32, name="warm")
+        nc.vector.memset(warm[:], 0.0)
+        nc.scalar.activation(out=warm[:], in_=warm[:], func=ACT.Identity)
+
+        for v, vector in enumerate((w_b, bn_gamma, bn_beta, bn_mean, bn_var)):
+            nc.scalar.dma_start(
+                out=vector_rows[CTILES * v : CTILES * (v + 1), :], in_=vector.rearrange("(i p) -> i p", p=P)
+            )
+        g_raw = []
+        a_raw = []
+        x_raw = []
+        w_codes = keep.tile([P, CHANNELS], U32, name="w_codes", align_bytes=64)
+        for n in range(BLOCKS + PROJECT_LAG):
+            if n < BLOCKS:
+                b, quarter = divmod(n, QUARTERS)
+                if quarter == 0:
+                    g_raw.append(keep.tile([P, PASSES, LANES, INNER], BF16, name="g_raw%d" % b))
+                    for g in range(PASSES):
+                        nc.sync.dma_start(
+                            out=g_raw[b][:, g],
+                            in_=g_x[b, g * K_PASS : (g + 1) * K_PASS, :].rearrange("(j l) c -> j l c", l=LANES),
+                        )
+                a_raw.append(keep.tile([P, 2, POINTS], BF16, name="a_raw%d" % n))
+                nc.sync.dma_start(
+                    out=a_raw[n][:],
+                    in_=affinity[b, quarter * QBLOCK : (quarter + 1) * QBLOCK, :].rearrange("(p r) s -> p r s", r=2),
+                )
+                if b == 0:
+                    nc.sync.dma_start(
+                        out=w_scales[32 * quarter : 32 * quarter + LANES, :].bitcast(I32),
+                        in_=w_w_scales[0, LANES * quarter : LANES * (quarter + 1), :].bitcast(I32),
+                    )
+            if n == PROJECT_LAG:
+                nc.sync.dma_start(
+                    out=w_codes[:].bitcast(I32), in_=w_w_words[0].rearrange("p n t -> p (n t)").bitcast(I32)
+                )
+            if n >= PROJECT_LAG:
+                b, quarter = divmod(n - PROJECT_LAG, QUARTERS)
+                x_raw.append(keep.tile([P, 2, POINTS], BF16, name="x_raw%d" % (n - PROJECT_LAG)))
+                nc.sync.dma_start(
+                    out=x_raw[-1][:],
+                    in_=x[b, quarter * 2 * P : (quarter + 1) * 2 * P, :].rearrange("(i p) q -> p i q", p=P),
+                )
+
+        vector_rows_f32 = keep.tile([P, P], F32, name="vector_rows_f32")
+        nc.gpsimd.tensor_copy(out=vector_rows_f32[:], in_=vector_rows[:])
+        gain = keep.tile([P, CTILES], F32, name="gain")
+        shift = keep.tile([P, CTILES], F32, name="shift")
+
+        g_grouped = {}
+        g_quantised = {}
+        a_grouped = {}
+        y_grouped = {}
+        y_quantised = {}
+        results = {}
+
+        def regroup_values(b):
+            g_grouped[b] = stage.tile([P, PASSES, INNER * LANES], BF16, name="g_grouped", bufs=1, align_bytes=64)
+            for g in range(PASSES):
+                nc.vector.tensor_copy(
+                    out=g_grouped[b][:, g, :].rearrange("j (l m s) -> j l m s", l=LANES, s=LANES),
+                    in_=g_raw[b][:, g].rearrange("j s (m l) -> j l m s", l=LANES),
+                )
+
+        def quantise_values(b):
+            g_codes = keep.tile([P, PASSES * INNER], U32, name="g_codes%d" % b, align_bytes=64)
+            g_scales = keep.tile([P, PASSES * INNER], U8, name="g_scales%d" % b, align_bytes=64)
+            nc.vector.quantize_mx(
+                out=g_codes[:].bitcast(FP8X4), scales=g_scales[:], in_=g_grouped[b][:].rearrange("j g c -> j (g c)")
+            )
+            g_quantised[b] = (g_codes, g_scales)
+
+        def transpose_block(n):
+            words = a_raw[n][:].bitcast(F32)
+            a_grouped[n] = stage.tile([P, PASSES, QBLOCK * LANES], BF16, name="a_grouped", align_bytes=64)
+            for g in range(PASSES):
+                turned = psum.tile([P, 2, 2, P], F32, name="turned", tag="bank")
+                for r in range(2):
+                    for u in range(2):
+                        every_second = words[:, r, g * 2 * P + u : (g + 1) * 2 * P : 2]
+                        nc.tensor.transpose(turned[:, r, u, :], every_second, identity[:])
+                nc.scalar.copy(
+                    out=a_grouped[n][:, g, :].bitcast(F32).rearrange("j (p r u) -> j p r u", r=2, u=2),
+                    in_=turned[:].rearrange("j r u p -> j p r u"),
+                )
+
+        def first_product(n):
+            b, quarter = divmod(n, QUARTERS)
+            half, part = divmod(quarter, QUARTERS // HALVES)
+            a_codes = stage.tile([P, PASSES * QBLOCK], U32, name="a_codes", align_bytes=64)
+            a_scales = stage.tile([P, PASSES * QBLOCK], U8, name="a_scales", align_bytes=64)
+            nc.vector.quantize_mx(
+                out=a_codes[:].bitcast(FP8X4), scales=a_scales[:], in_=a_grouped[n][:].rearrange("j g c -> j (g c)")
+            )
+            if quarter == QUARTERS - QUANTISE_AHEAD and b + 1 < BATCH:
+                quantise_values(b + 1)
+            g_codes, g_scales = g_quantised[b]
+            if part == 0:
+                y_grouped[b, half] = stage.tile([P, BANK, LANES], BF16, name="y_grouped", align_bytes=64)
+            for k in range(QBLOCK // P):
+                sums = psum.tile([P, LANES, P], F32, name="sums", tag="bank")
+                for l in range(LANES):
+                    for g in range(PASSES):
+                        stationary = slice(g * INNER + l * P, g * INNER + (l + 1) * P)
+                        moving = slice(g * QBLOCK + k * P, g * QBLOCK + (k + 1) * P)
+                        nc.tensor.matmul_mx(
+                            out=sums[:, l, :],
+                            lhsT=g_codes[:, stationary].bitcast(FP8X4),
+                            lhsT_scale=g_scales[:, stationary],
+                            rhs=a_codes[:, moving].bitcast(FP8X4),
+                            rhs_scale=a_scales[:, moving],
+                            start=(g == 0),
+                            stop=(g == PASSES - 1),
+                        )
+                first = part * QBLOCK + k * P
+                nc.scalar.copy(out=y_grouped[b, half][:, first : first + P, :], in_=sums[:].rearrange("m l q -> m q l"))
+            if part == QUARTERS // HALVES - 1:
+                y_codes = keep.tile([P, BANK], U32, name="y_codes%d_%d" % (b, half), align_bytes=64)
+                y_scales = keep.tile([P, BANK], U8, name="y_scales%d_%d" % (b, half), align_bytes=64)
+                nc.vector.quantize_mx(
+                    out=y_codes[:].bitcast(FP8X4),
+                    scales=y_scales[:],
+                    in_=y_grouped[b, half][:].rearrange("m q l -> m (q l)"),
+                )
+                y_quantised[b, half] = (y_codes, y_scales)
+
+        def make_gain_and_shift():
+            turned_vectors = psum.tile([P, BANK], F32, name="turned_vectors", tag="bank")
+            nc.tensor.transpose(turned_vectors[:, 0:P], vector_rows_f32[:], identity[:])
+            per_channel = keep.tile([P, 5, CTILES], F32, name="per_channel")
+            nc.scalar.copy(out=per_channel[:].rearrange("p v i -> p (v i)"), in_=turned_vectors[:, 0 : 5 * CTILES])
+            bias_c, gamma_c, beta_c, mean_c, var_c = [per_channel[:, v, :] for v in range(5)]
+            nc.gpsimd.tensor_scalar(out=gain[:], in0=var_c, scalar1=1.0, scalar2=EPS, op0=ALU.mult, op1=ALU.add)
+            nc.gpsimd.tensor_tensor(out=gain[:], in0=gain[:], in1=minus_half[:], op=ALU.pow)
+            nc.gpsimd.tensor_tensor(out=gain[:], in0=gain[:], in1=gamma_c, op=ALU.mult)
+            nc.gpsimd.tensor_tensor(out=shift[:], in0=bias_c, in1=mean_c, op=ALU.subtract)
+            nc.gpsimd.tensor_tensor(out=shift[:], in0=shift[:], in1=gain[:], op=ALU.mult)
+            nc.gpsimd.tensor_tensor(out=shift[:], in0=shift[:], in1=beta_c, op=ALU.add)
+
+        def add_shift(n):
+            b, quarter = divmod(n, QUARTERS)
+            even, odd = 2 * quarter, 2 * quarter + 1
+            results[b, even] = keep.tile([P, POINTS], F32, name="result%d_%d" % (b, even))
+            results[b, odd] = keep.tile([P, POINTS], F32, name="result%d_%d" % (b, odd))
+            nc.scalar.activation(
+                out=results[b, even][:], in_=x_raw[n][:, 0, :], func=ACT.Identity, bias=shift[:, even : even + 1]
+            )
+            nc.gpsimd.tensor_scalar(
+                out=results[b, odd][:],
+                in0=x_raw[n][:, 1, :],
+                scalar1=1.0,
+                scalar2=shift[:, odd : odd + 1],
+                op0=ALU.mult,
+                op1=ALU.add,
+            )
+
+        def second_product(n):
+            b, quarter = divmod(n, QUARTERS)
+            for i in (2 * quarter, 2 * quarter + 1):
+                channels = slice(i * P, (i + 1) * P)
+                for half in range(HALVES):
+                    points = slice(half * BANK, (half + 1) * BANK)
+                    y_codes, y_scales = y_quantised[b, half]
+                    projected = psum.tile([P, BANK], F32, name="projected", tag="bank")
+                    nc.tensor.matmul_mx(
+                        out=projected[:],
+                        lhsT=w_codes[:, channels].bitcast(FP8X4),
+                        lhsT_scale=w_scales[:, channels],
+                        rhs=y_codes[:].bitcast(FP8X4),
+                        rhs_scale=y_scales[:],
+                        start=True,
+                        stop=True,
+                    )
+                    nc.vector.scalar_tensor_tensor(
+                        out=results[b, i][:, points],
+                        in0=projected[:],
+                        scalar=gain[:, i : i + 1],
+                        in1=results[b, i][:, points],
+                        op0=ALU.mult,
+                        op1=ALU.add,
+                    )
+                nc.sync.dma_start(out=out[b, channels, :], in_=results[b, i][:])
+
+        regroup_values(0)
+        quantise_values(0)
+        transpose_block(0)
+        for step in range(BLOCKS + PROJECT_LAG):
+            if step + TURN_AHEAD < BLOCKS:
+                transpose_block(step + TURN_AHEAD)
+            if step < BLOCKS:
+                first_product(step)
+            if (step + REGROUP_AHEAD) % QUARTERS == 0 and step + REGROUP_AHEAD < BLOCKS:
+                regroup_values((step + REGROUP_AHEAD) // QUARTERS)
+            if step == GAIN_STEP:
+                make_gain_and_shift()
+            if 0 <= step - SHIFT_LAG < BLOCKS:
+                add_shift(step - SHIFT_LAG)
+            if 0 <= step - PROJECT_LAG:
+                second_product(step - PROJECT_LAG)

@@ -30,13 +30,10 @@ BLOCKS = BATCH * QUARTERS
 HALVES = POINTS // BANK
 CTILES = CHANNELS // P
 
-TURN_AHEAD = 1
-REGROUP_AHEAD = 2
-QUANTISE_AHEAD = 1
-PROJECT_LAG = QUARTERS
-SHIFT_LAG = PROJECT_LAG - 1
-GAIN_STEP = SHIFT_LAG - 2
+KINDS = ("GSGSGSGS","GSCGCGSG")
 
+UNITS = (0, 0, 2, 2, 4, 4, 4, 0)
+SHIFTS = (0, 0, 2, 2, 2, 2, 2, 2)
 FLOPS = 2 * BATCH * (POINTS * POINTS * INNER + CHANNELS * INNER * POINTS)
 
 
@@ -47,89 +44,111 @@ def tile_sgcam_pb_kernel(
     with ExitStack() as ctx:
         keep = ctx.enter_context(tc.tile_pool(name="keep", bufs=1))
         stage = ctx.enter_context(tc.tile_pool(name="stage", bufs=3))
+        ctx.enter_context(tc.manual_schedule())
         psum = ctx.enter_context(tc.psum_pool(name="psum", bufs=8))
 
         identity = keep.tile([P, P], F32, name="identity")
         make_identity(nc, identity[:])
-        minus_half = keep.tile([P, CTILES], F32, name="minus_half")
-        nc.gpsimd.memset(minus_half[:], -0.5)
-        w_scales = keep.tile([P, CHANNELS], U8, name="w_scales", align_bytes=64)
-        nc.vector.memset(w_scales[:].bitcast(I32), 0)
         vector_rows = keep.tile([P, P], BF16, name="vector_rows")
         nc.vector.memset(vector_rows[:], 0.0)
-        warm = keep.tile([P, 1], F32, name="warm")
-        nc.vector.memset(warm[:], 0.0)
-        nc.scalar.activation(out=warm[:], in_=warm[:], func=ACT.Identity)
-
+        w_scales = keep.tile([P, CHANNELS], U8, name="w_scales", align_bytes=64)
+        nc.vector.memset(w_scales[:].bitcast(I32), 0)
         for v, vector in enumerate((w_b, bn_gamma, bn_beta, bn_mean, bn_var)):
             nc.scalar.dma_start(
                 out=vector_rows[CTILES * v : CTILES * (v + 1), :], in_=vector.rearrange("(i p) -> i p", p=P)
             )
-        g_raw = []
-        a_raw = []
-        x_raw = []
+        warm = keep.tile([P, 1], F32, name="warm")
+        nc.vector.memset(warm[:], 0.0)
+        nc.scalar.activation(out=warm[:], in_=warm[:], func=ACT.Sqrt)
+        g_raw = {}
+        a_raw = {}
+        x_raw = {}
         w_codes = keep.tile([P, CHANNELS], U32, name="w_codes", align_bytes=64)
-        for n in range(BLOCKS + PROJECT_LAG):
-            if n < BLOCKS:
-                b, quarter = divmod(n, QUARTERS)
-                if quarter == 0:
-                    g_raw.append(keep.tile([P, PASSES, LANES, INNER], BF16, name="g_raw%d" % b))
-                    for g in range(PASSES):
-                        nc.sync.dma_start(
-                            out=g_raw[b][:, g],
-                            in_=g_x[b, g * K_PASS : (g + 1) * K_PASS, :].rearrange("(j l) c -> j l c", l=LANES),
-                        )
-                a_raw.append(keep.tile([P, 2, POINTS], BF16, name="a_raw%d" % n))
-                nc.sync.dma_start(
-                    out=a_raw[n][:],
-                    in_=affinity[b, quarter * QBLOCK : (quarter + 1) * QBLOCK, :].rearrange("(p r) s -> p r s", r=2),
-                )
-                if b == 0:
-                    nc.sync.dma_start(
-                        out=w_scales[32 * quarter : 32 * quarter + LANES, :].bitcast(I32),
-                        in_=w_w_scales[0, LANES * quarter : LANES * (quarter + 1), :].bitcast(I32),
-                    )
-            if n == PROJECT_LAG:
-                nc.sync.dma_start(
-                    out=w_codes[:].bitcast(I32), in_=w_w_words[0].rearrange("p n t -> p (n t)").bitcast(I32)
-                )
-            if n >= PROJECT_LAG:
-                b, quarter = divmod(n - PROJECT_LAG, QUARTERS)
-                x_raw.append(keep.tile([P, 2, POINTS], BF16, name="x_raw%d" % (n - PROJECT_LAG)))
-                nc.sync.dma_start(
-                    out=x_raw[-1][:],
-                    in_=x[b, quarter * 2 * P : (quarter + 1) * 2 * P, :].rearrange("(i p) q -> p i q", p=P),
-                )
+
+        def load_values(b, g):
+            if g == 0:
+                g_raw[b] = keep.tile([P, PASSES, LANES, INNER], BF16, name="g_raw%d" % b)
+            nc.sync.dma_start(
+                out=g_raw[b][:, g],
+                in_=g_x[b, g * K_PASS : (g + 1) * K_PASS, :].rearrange("(j l) c -> j l c", l=LANES),
+            )
+
+        def load_affinity(n):
+            b, quarter = divmod(n, QUARTERS)
+            a_raw[n] = keep.tile([P, 2, POINTS], BF16, name="a_raw%d" % n)
+            nc.sync.dma_start(
+                out=a_raw[n][:],
+                in_=affinity[b, quarter * QBLOCK : (quarter + 1) * QBLOCK, :].rearrange("(p r) s -> p r s", r=2),
+            )
+
+        def load_weight_scales(Q):
+            nc.sync.dma_start(
+                out=w_scales[32 * Q : 32 * Q + LANES, :].bitcast(I32),
+                in_=w_w_scales[0, LANES * Q : LANES * (Q + 1), :].bitcast(I32),
+            )
+
+        def load_residual(n):
+            b, quarter = divmod(n, QUARTERS)
+            x_raw[n] = keep.tile([P, 2, POINTS], BF16, name="x_raw%d" % n)
+            nc.sync.dma_start(
+                out=x_raw[n][:],
+                in_=x[b, quarter * 2 * P : (quarter + 1) * 2 * P, :].rearrange("(i p) q -> p i q", p=P),
+            )
+
+        load_values(0, 0)
+        load_affinity(0)
+        load_values(0, 1)
+        load_affinity(1)
+        load_values(1, 0)
+        for Q in range(LANES):
+            load_weight_scales(Q)
+        load_affinity(2)
+        load_values(1, 1)
+        load_affinity(3)
+        nc.sync.dma_start(out=w_codes[:].bitcast(I32), in_=w_w_words[0].rearrange("p n t -> p (n t)").bitcast(I32))
+        load_residual(0)
+        for n in range(QUARTERS, BLOCKS):
+            load_affinity(n)
+            load_residual(n - QUARTERS + 1)
+        for n in range(QUARTERS + 1, BLOCKS):
+            load_residual(n)
 
         vector_rows_f32 = keep.tile([P, P], F32, name="vector_rows_f32")
-        nc.gpsimd.tensor_copy(out=vector_rows_f32[:], in_=vector_rows[:])
         gain = keep.tile([P, CTILES], F32, name="gain")
+        deviation = keep.tile([P, CTILES], F32, name="deviation")
         shift = keep.tile([P, CTILES], F32, name="shift")
 
         g_grouped = {}
         g_quantised = {}
         a_grouped = {}
+        a_quantised = {}
         y_grouped = {}
         y_quantised = {}
         results = {}
+        copy_on = {"V": nc.vector.tensor_copy, "S": nc.scalar.copy}
 
-        def regroup_values(b):
-            g_grouped[b] = stage.tile([P, PASSES, INNER * LANES], BF16, name="g_grouped", bufs=1, align_bytes=64)
-            for g in range(PASSES):
-                nc.vector.tensor_copy(
-                    out=g_grouped[b][:, g, :].rearrange("j (l m s) -> j l m s", l=LANES, s=LANES),
-                    in_=g_raw[b][:, g].rearrange("j s (m l) -> j l m s", l=LANES),
-                )
-
-        def quantise_values(b):
-            g_codes = keep.tile([P, PASSES * INNER], U32, name="g_codes%d" % b, align_bytes=64)
-            g_scales = keep.tile([P, PASSES * INNER], U8, name="g_scales%d" % b, align_bytes=64)
-            nc.vector.quantize_mx(
-                out=g_codes[:].bitcast(FP8X4), scales=g_scales[:], in_=g_grouped[b][:].rearrange("j g c -> j (g c)")
+        def regroup_values(b, g, engine):
+            if g == 0:
+                g_grouped[b] = stage.tile([P, PASSES, INNER * LANES], BF16, name="g_grouped", bufs=1, align_bytes=64)
+            copy_on[engine](
+                out=g_grouped[b][:, g, :].rearrange("j (l m s) -> j l m s", l=LANES, s=LANES),
+                in_=g_raw[b][:, g].rearrange("j s (m l) -> j l m s", l=LANES),
             )
-            g_quantised[b] = (g_codes, g_scales)
 
-        def transpose_block(n):
+        def quantise_values(b, g):
+            if g == 0:
+                g_quantised[b] = (
+                    keep.tile([P, PASSES * INNER], U32, name="g_codes%d" % b, align_bytes=64),
+                    keep.tile([P, PASSES * INNER], U8, name="g_scales%d" % b, align_bytes=64),
+                )
+            columns = slice(g * INNER, (g + 1) * INNER)
+            nc.vector.quantize_mx(
+                out=g_quantised[b][0][:, columns].bitcast(FP8X4),
+                scales=g_quantised[b][1][:, columns],
+                in_=g_grouped[b][:, g, :],
+            )
+
+        def transpose_block(n, engines="SS"):
             words = a_raw[n][:].bitcast(F32)
             a_grouped[n] = stage.tile([P, PASSES, QBLOCK * LANES], BF16, name="a_grouped", align_bytes=64)
             for g in range(PASSES):
@@ -138,21 +157,23 @@ def tile_sgcam_pb_kernel(
                     for u in range(2):
                         every_second = words[:, r, g * 2 * P + u : (g + 1) * 2 * P : 2]
                         nc.tensor.transpose(turned[:, r, u, :], every_second, identity[:])
-                nc.scalar.copy(
+                copy_on[engines[g]](
                     out=a_grouped[n][:, g, :].bitcast(F32).rearrange("j (p r u) -> j p r u", r=2, u=2),
                     in_=turned[:].rearrange("j r u p -> j p r u"),
                 )
 
-        def first_product(n):
-            b, quarter = divmod(n, QUARTERS)
-            half, part = divmod(quarter, QUARTERS // HALVES)
+        def quantise_affinity(n):
             a_codes = stage.tile([P, PASSES * QBLOCK], U32, name="a_codes", align_bytes=64)
             a_scales = stage.tile([P, PASSES * QBLOCK], U8, name="a_scales", align_bytes=64)
             nc.vector.quantize_mx(
                 out=a_codes[:].bitcast(FP8X4), scales=a_scales[:], in_=a_grouped[n][:].rearrange("j g c -> j (g c)")
             )
-            if quarter == QUARTERS - QUANTISE_AHEAD and b + 1 < BATCH:
-                quantise_values(b + 1)
+            a_quantised[n] = (a_codes, a_scales)
+
+        def first_product(n, engines="SS"):
+            b, quarter = divmod(n, QUARTERS)
+            half, part = divmod(quarter, QUARTERS // HALVES)
+            a_codes, a_scales = a_quantised[n]
             g_codes, g_scales = g_quantised[b]
             if part == 0:
                 y_grouped[b, half] = stage.tile([P, BANK, LANES], BF16, name="y_grouped", align_bytes=64)
@@ -172,87 +193,106 @@ def tile_sgcam_pb_kernel(
                             stop=(g == PASSES - 1),
                         )
                 first = part * QBLOCK + k * P
-                nc.scalar.copy(out=y_grouped[b, half][:, first : first + P, :], in_=sums[:].rearrange("m l q -> m q l"))
-            if part == QUARTERS // HALVES - 1:
-                y_codes = keep.tile([P, BANK], U32, name="y_codes%d_%d" % (b, half), align_bytes=64)
-                y_scales = keep.tile([P, BANK], U8, name="y_scales%d_%d" % (b, half), align_bytes=64)
-                nc.vector.quantize_mx(
-                    out=y_codes[:].bitcast(FP8X4),
-                    scales=y_scales[:],
-                    in_=y_grouped[b, half][:].rearrange("m q l -> m (q l)"),
+                copy_on[engines[k]](
+                    out=y_grouped[b, half][:, first : first + P, :], in_=sums[:].rearrange("m l q -> m q l")
                 )
-                y_quantised[b, half] = (y_codes, y_scales)
+
+        def quantise_y(b, half):
+            y_codes = keep.tile([P, BANK], U32, name="y_codes%d_%d" % (b, half), align_bytes=64)
+            y_scales = keep.tile([P, BANK], U8, name="y_scales%d_%d" % (b, half), align_bytes=64)
+            nc.vector.quantize_mx(
+                out=y_codes[:].bitcast(FP8X4),
+                scales=y_scales[:],
+                in_=y_grouped[b, half][:].rearrange("m q l -> m (q l)"),
+            )
+            y_quantised[b, half] = (y_codes, y_scales)
 
         def make_gain_and_shift():
+            nc.scalar.copy(out=vector_rows_f32[:], in_=vector_rows[:])
             turned_vectors = psum.tile([P, BANK], F32, name="turned_vectors", tag="bank")
             nc.tensor.transpose(turned_vectors[:, 0:P], vector_rows_f32[:], identity[:])
             per_channel = keep.tile([P, 5, CTILES], F32, name="per_channel")
             nc.scalar.copy(out=per_channel[:].rearrange("p v i -> p (v i)"), in_=turned_vectors[:, 0 : 5 * CTILES])
             bias_c, gamma_c, beta_c, mean_c, var_c = [per_channel[:, v, :] for v in range(5)]
-            nc.gpsimd.tensor_scalar(out=gain[:], in0=var_c, scalar1=1.0, scalar2=EPS, op0=ALU.mult, op1=ALU.add)
-            nc.gpsimd.tensor_tensor(out=gain[:], in0=gain[:], in1=minus_half[:], op=ALU.pow)
-            nc.gpsimd.tensor_tensor(out=gain[:], in0=gain[:], in1=gamma_c, op=ALU.mult)
-            nc.gpsimd.tensor_tensor(out=shift[:], in0=bias_c, in1=mean_c, op=ALU.subtract)
-            nc.gpsimd.tensor_tensor(out=shift[:], in0=shift[:], in1=gain[:], op=ALU.mult)
-            nc.gpsimd.tensor_tensor(out=shift[:], in0=shift[:], in1=beta_c, op=ALU.add)
+            nc.vector.tensor_scalar(out=gain[:], in0=var_c, scalar1=EPS, scalar2=None, op0=ALU.add)
+            nc.scalar.activation(out=deviation[:], in_=gain[:], func=ACT.Sqrt)
+            nc.vector.tensor_tensor(out=shift[:], in0=bias_c, in1=mean_c, op=ALU.subtract)
+            nc.vector.reciprocal(out=gain[:], in_=deviation[:])
+            nc.vector.tensor_tensor(out=gain[:], in0=gain[:], in1=gamma_c, op=ALU.mult)
+            nc.vector.tensor_tensor(out=shift[:], in0=shift[:], in1=gain[:], op=ALU.mult)
+            nc.vector.tensor_tensor(out=shift[:], in0=shift[:], in1=beta_c, op=ALU.add)
 
-        def add_shift(n):
-            b, quarter = divmod(n, QUARTERS)
-            even, odd = 2 * quarter, 2 * quarter + 1
-            results[b, even] = keep.tile([P, POINTS], F32, name="result%d_%d" % (b, even))
-            results[b, odd] = keep.tile([P, POINTS], F32, name="result%d_%d" % (b, odd))
-            nc.scalar.activation(
-                out=results[b, even][:], in_=x_raw[n][:, 0, :], func=ACT.Identity, bias=shift[:, even : even + 1]
-            )
-            nc.gpsimd.tensor_scalar(
-                out=results[b, odd][:],
-                in0=x_raw[n][:, 1, :],
-                scalar1=1.0,
-                scalar2=shift[:, odd : odd + 1],
-                op0=ALU.mult,
-                op1=ALU.add,
-            )
+        def add_shift(b, i):
+            residual = x_raw[b * QUARTERS + i // 2][:, i % 2, :]
+            if KINDS[b][i] == "C":
+                return
+            results[b, i] = keep.tile([P, POINTS], F32, name="result%d_%d" % (b, i))
+            if KINDS[b][i] == "S":
+                nc.scalar.activation(out=results[b, i][:], in_=residual, func=ACT.Identity, bias=shift[:, i : i + 1])
+            else:
+                nc.gpsimd.tensor_scalar(
+                    out=results[b, i][:], in0=residual, scalar1=1.0, scalar2=shift[:, i : i + 1], op0=ALU.mult, op1=ALU.add
+                )
 
-        def second_product(n):
-            b, quarter = divmod(n, QUARTERS)
-            for i in (2 * quarter, 2 * quarter + 1):
-                channels = slice(i * P, (i + 1) * P)
-                for half in range(HALVES):
-                    points = slice(half * BANK, (half + 1) * BANK)
-                    y_codes, y_scales = y_quantised[b, half]
-                    projected = psum.tile([P, BANK], F32, name="projected", tag="bank")
-                    nc.tensor.matmul_mx(
-                        out=projected[:],
-                        lhsT=w_codes[:, channels].bitcast(FP8X4),
-                        lhsT_scale=w_scales[:, channels],
-                        rhs=y_codes[:].bitcast(FP8X4),
-                        rhs_scale=y_scales[:],
-                        start=True,
-                        stop=True,
-                    )
-                    nc.vector.scalar_tensor_tensor(
-                        out=results[b, i][:, points],
-                        in0=projected[:],
-                        scalar=gain[:, i : i + 1],
-                        in1=results[b, i][:, points],
-                        op0=ALU.mult,
-                        op1=ALU.add,
-                    )
+        def second_product(b, half, i):
+            channels = slice(i * P, (i + 1) * P)
+            points = slice(half * BANK, (half + 1) * BANK)
+            y_codes, y_scales = y_quantised[b, half]
+            projected = psum.tile([P, BANK], F32, name="projected", tag="bank")
+            nc.tensor.matmul_mx(
+                out=projected[:],
+                lhsT=w_codes[:, channels].bitcast(FP8X4),
+                lhsT_scale=w_scales[:, channels],
+                rhs=y_codes[:].bitcast(FP8X4),
+                rhs_scale=y_scales[:],
+                start=True,
+                stop=True,
+            )
+            if (b, i) not in results:
+                results[b, i] = keep.tile([P, POINTS], F32, name="result%d_%d" % (b, i))
+            target = results[b, i][:, points]
+            if KINDS[b][i] == "C":
+                nc.scalar.activation(
+                    out=target, in_=projected[:], func=ACT.Identity, scale=gain[:, i : i + 1], bias=shift[:, i : i + 1]
+                )
+                residual = x_raw[b * QUARTERS + i // 2][:, i % 2, points]
+                nc.gpsimd.tensor_tensor(out=target, in0=target, in1=residual, op=ALU.add)
+            else:
+                nc.vector.scalar_tensor_tensor(
+                    out=target, in0=projected[:], scalar=gain[:, i : i + 1], in1=target, op0=ALU.mult, op1=ALU.add
+                )
+            if half == HALVES - 1:
                 nc.sync.dma_start(out=out[b, channels, :], in_=results[b, i][:])
 
-        regroup_values(0)
-        quantise_values(0)
+        make_gain_and_shift()
+        regroup_values(0, 0, "V")
         transpose_block(0)
-        for step in range(BLOCKS + PROJECT_LAG):
-            if step + TURN_AHEAD < BLOCKS:
-                transpose_block(step + TURN_AHEAD)
-            if step < BLOCKS:
-                first_product(step)
-            if (step + REGROUP_AHEAD) % QUARTERS == 0 and step + REGROUP_AHEAD < BLOCKS:
-                regroup_values((step + REGROUP_AHEAD) // QUARTERS)
-            if step == GAIN_STEP:
-                make_gain_and_shift()
-            if 0 <= step - SHIFT_LAG < BLOCKS:
-                add_shift(step - SHIFT_LAG)
-            if 0 <= step - PROJECT_LAG:
-                second_product(step - PROJECT_LAG)
+        quantise_values(0, 0)
+        regroup_values(0, 1, "V")
+        quantise_affinity(0)
+        quantise_values(0, 1)
+        transpose_block(1)
+        units = [(0, half, i) for half in range(HALVES) for i in range(4)]
+        units += [(0, half, i) for i in range(4, CTILES) for half in range(HALVES)]
+        units += [(1, half, i) for i in range(CTILES) for half in range(HALVES)]
+        shifts = [(b, i) for b in range(BATCH) for i in range(CTILES)]
+        for n in range(BLOCKS):
+            if n in (0, 1):
+                regroup_values(1, n, "V")
+            if n + 1 < BLOCKS:
+                quantise_affinity(n + 1)
+            first_product(n, "SS")
+            if n in (0, 1):
+                quantise_values(1, n)
+            for k in range(SHIFTS[n]):
+                add_shift(*shifts.pop(0))
+            for k in range(UNITS[n]):
+                second_product(*units.pop(0))
+            if n + 2 < BLOCKS:
+                transpose_block(n + 2)
+            if n % 2:
+                quantise_y(n // QUARTERS, n % QUARTERS // 2)
+        for b, i in shifts:
+            add_shift(b, i)
+        for unit in units:
+            second_product(*unit)

@@ -30,7 +30,7 @@ BLOCKS = BATCH * QUARTERS
 HALVES = POINTS // BANK
 CTILES = CHANNELS // P
 
-KINDS = ("GSGSGSGS","GSCGCGSG")
+KINDS = ("GGGSGSGS","GSCGCGSG")
 
 UNITS = (0, 0, 2, 2, 4, 4, 4, 0)
 SHIFTS = (0, 0, 2, 2, 2, 2, 2, 2)
@@ -51,6 +51,8 @@ def tile_sgcam_pb_kernel(
         make_identity(nc, identity[:])
         vector_rows = keep.tile([P, P], BF16, name="vector_rows")
         nc.vector.memset(vector_rows[:], 0.0)
+        epsilon = keep.tile([P, 1], F32, name="epsilon")
+        nc.gpsimd.memset(epsilon[:], EPS)
         w_scales = keep.tile([P, CHANNELS], U8, name="w_scales", align_bytes=64)
         nc.vector.memset(w_scales[:].bitcast(I32), 0)
         for v, vector in enumerate((w_b, bn_gamma, bn_beta, bn_mean, bn_var)):
@@ -214,8 +216,10 @@ def tile_sgcam_pb_kernel(
             per_channel = keep.tile([P, 5, CTILES], F32, name="per_channel")
             nc.scalar.copy(out=per_channel[:].rearrange("p v i -> p (v i)"), in_=turned_vectors[:, 0 : 5 * CTILES])
             bias_c, gamma_c, beta_c, mean_c, var_c = [per_channel[:, v, :] for v in range(5)]
-            nc.vector.tensor_scalar(out=gain[:], in0=var_c, scalar1=EPS, scalar2=None, op0=ALU.add)
-            nc.scalar.activation(out=deviation[:], in_=gain[:], func=ACT.Sqrt)
+            nc.scalar.activation(out=deviation[:], in_=var_c, func=ACT.Sqrt, bias=epsilon[:])
+            return bias_c, gamma_c, beta_c, mean_c
+
+        def finish_gain_and_shift(bias_c, gamma_c, beta_c, mean_c):
             nc.vector.tensor_tensor(out=shift[:], in0=bias_c, in1=mean_c, op=ALU.subtract)
             nc.vector.reciprocal(out=gain[:], in_=deviation[:])
             nc.vector.tensor_tensor(out=gain[:], in0=gain[:], in1=gamma_c, op=ALU.mult)
@@ -264,14 +268,15 @@ def tile_sgcam_pb_kernel(
             if half == HALVES - 1:
                 nc.sync.dma_start(out=out[b, channels, :], in_=results[b, i][:])
 
-        make_gain_and_shift()
         regroup_values(0, 0, "V")
         transpose_block(0)
         quantise_values(0, 0)
         regroup_values(0, 1, "V")
+        vectors = make_gain_and_shift()
         quantise_affinity(0)
         quantise_values(0, 1)
         transpose_block(1)
+        finish_gain_and_shift(*vectors)
         units = [(0, half, i) for half in range(HALVES) for i in range(4)]
         units += [(0, half, i) for i in range(4, CTILES) for half in range(HALVES)]
         units += [(1, half, i) for i in range(CTILES) for half in range(HALVES)]

@@ -30,7 +30,7 @@ BLOCKS = BATCH * QUARTERS
 HALVES = POINTS // BANK
 CTILES = CHANNELS // P
 
-KINDS = ("GGGSGSGS","GSCGCGSG")
+KINDS = (("G", "G", "G", "S", "G", "S", "G", "S"), ("G", "S", "G", "S", "C", "G", "C", "G"))
 
 UNITS = (0, 0, 2, 2, 4, 4, 4, 0)
 SHIFTS = (0, 0, 2, 2, 2, 2, 2, 2)
@@ -116,6 +116,8 @@ def tile_sgcam_pb_kernel(
             load_residual(n)
 
         vector_rows_f32 = keep.tile([P, P], F32, name="vector_rows_f32")
+        per_channel = keep.tile([P, 5, CTILES], F32, name="per_channel")
+        bias_c, gamma_c, beta_c, mean_c, var_c = [per_channel[:, v, :] for v in range(5)]
         gain = keep.tile([P, CTILES], F32, name="gain")
         deviation = keep.tile([P, CTILES], F32, name="deviation")
         shift = keep.tile([P, CTILES], F32, name="shift")
@@ -210,16 +212,13 @@ def tile_sgcam_pb_kernel(
             y_quantised[b, half] = (y_codes, y_scales)
 
         def make_gain_and_shift():
-            nc.scalar.copy(out=vector_rows_f32[:], in_=vector_rows[:])
+            nc.vector.tensor_copy(out=vector_rows_f32[:], in_=vector_rows[:])
             turned_vectors = psum.tile([P, BANK], F32, name="turned_vectors", tag="bank")
             nc.tensor.transpose(turned_vectors[:, 0:P], vector_rows_f32[:], identity[:])
-            per_channel = keep.tile([P, 5, CTILES], F32, name="per_channel")
             nc.scalar.copy(out=per_channel[:].rearrange("p v i -> p (v i)"), in_=turned_vectors[:, 0 : 5 * CTILES])
-            bias_c, gamma_c, beta_c, mean_c, var_c = [per_channel[:, v, :] for v in range(5)]
             nc.scalar.activation(out=deviation[:], in_=var_c, func=ACT.Sqrt, bias=epsilon[:])
-            return bias_c, gamma_c, beta_c, mean_c
 
-        def finish_gain_and_shift(bias_c, gamma_c, beta_c, mean_c):
+        def finish_gain_and_shift():
             nc.vector.tensor_tensor(out=shift[:], in0=bias_c, in1=mean_c, op=ALU.subtract)
             nc.vector.reciprocal(out=gain[:], in_=deviation[:])
             nc.vector.tensor_tensor(out=gain[:], in0=gain[:], in1=gamma_c, op=ALU.mult)
@@ -272,11 +271,9 @@ def tile_sgcam_pb_kernel(
         transpose_block(0)
         quantise_values(0, 0)
         regroup_values(0, 1, "V")
-        vectors = make_gain_and_shift()
         quantise_affinity(0)
         quantise_values(0, 1)
         transpose_block(1)
-        finish_gain_and_shift(*vectors)
         units = [(0, half, i) for half in range(HALVES) for i in range(4)]
         units += [(0, half, i) for i in range(4, CTILES) for half in range(HALVES)]
         units += [(1, half, i) for i in range(CTILES) for half in range(HALVES)]
@@ -289,12 +286,16 @@ def tile_sgcam_pb_kernel(
             first_product(n, "SS")
             if n in (0, 1):
                 quantise_values(1, n)
+            if n == 1:
+                finish_gain_and_shift()
             for k in range(SHIFTS[n]):
                 add_shift(*shifts.pop(0))
             for k in range(UNITS[n]):
                 second_product(*units.pop(0))
             if n + 2 < BLOCKS:
                 transpose_block(n + 2)
+            if n == 0:
+                make_gain_and_shift()
             if n % 2:
                 quantise_y(n // QUARTERS, n % QUARTERS // 2)
         for b, i in shifts:

@@ -135,8 +135,8 @@ def tile_sgcam_pb_kernel(
             if g == 0:
                 g_grouped[b] = stage.tile([P, PASSES, INNER * LANES], BF16, name="g_grouped", bufs=1, align_bytes=64)
             copy_on[engine](
-                out=g_grouped[b][:, g, :].rearrange("j (l m s) -> j l m s", l=LANES, s=LANES),
-                in_=g_raw[b][:, g].rearrange("j s (m l) -> j l m s", l=LANES),
+                out=g_grouped[b][:, g, :].rearrange("j (l m i s) -> j l m s i", l=LANES, i=4, s=LANES),
+                in_=g_raw[b][:, g].rearrange("j s (m i l) -> j l m s i", i=4, l=LANES),
             )
 
         def quantise_values(b, g):

@@ -30,7 +30,7 @@ BLOCKS = BATCH * QUARTERS
 HALVES = POINTS // BANK
 CTILES = CHANNELS // P
 
-KINDS = (("G", "G", "G", "S", "G", "S", "G", "S"), ("G", "S", "G", "S", "C", "G", "C", "G"))
+KINDS = (("G", "G", "G", "S", "G", "S", "G", "S"), ("G", "S", "C", "G", "S", "C", "G", "S"))
 
 UNITS = (0, 0, 2, 2, 4, 4, 4, 0)
 SHIFTS = (0, 0, 2, 2, 2, 2, 2, 2)
@@ -211,19 +211,26 @@ def tile_sgcam_pb_kernel(
             )
             y_quantised[b, half] = (y_codes, y_scales)
 
-        def make_gain_and_shift():
+        def cast_vectors():
             nc.vector.tensor_copy(out=vector_rows_f32[:], in_=vector_rows[:])
+
+        def turn_vectors():
             turned_vectors = psum.tile([P, BANK], F32, name="turned_vectors", tag="bank")
             nc.tensor.transpose(turned_vectors[:, 0:P], vector_rows_f32[:], identity[:])
             nc.scalar.copy(out=per_channel[:].rearrange("p v i -> p (v i)"), in_=turned_vectors[:, 0 : 5 * CTILES])
             nc.scalar.activation(out=deviation[:], in_=var_c, func=ACT.Sqrt, bias=epsilon[:])
 
-        def finish_gain_and_shift():
-            nc.vector.tensor_tensor(out=shift[:], in0=bias_c, in1=mean_c, op=ALU.subtract)
-            nc.vector.reciprocal(out=gain[:], in_=deviation[:])
-            nc.vector.tensor_tensor(out=gain[:], in0=gain[:], in1=gamma_c, op=ALU.mult)
-            nc.vector.tensor_tensor(out=shift[:], in0=shift[:], in1=gain[:], op=ALU.mult)
-            nc.vector.tensor_tensor(out=shift[:], in0=shift[:], in1=beta_c, op=ALU.add)
+        def gain_and_shift(step):
+            if step == 0:
+                nc.vector.tensor_tensor(out=shift[:], in0=bias_c, in1=mean_c, op=ALU.subtract)
+            elif step == 1:
+                nc.vector.reciprocal(out=gain[:], in_=deviation[:])
+            elif step == 2:
+                nc.vector.tensor_tensor(out=gain[:], in0=gain[:], in1=gamma_c, op=ALU.mult)
+            elif step == 3:
+                nc.vector.tensor_tensor(out=shift[:], in0=shift[:], in1=gain[:], op=ALU.mult)
+            else:
+                nc.vector.tensor_tensor(out=shift[:], in0=shift[:], in1=beta_c, op=ALU.add)
 
         def add_shift(b, i):
             residual = x_raw[b * QUARTERS + i // 2][:, i % 2, :]
@@ -265,7 +272,16 @@ def tile_sgcam_pb_kernel(
                     out=target, in0=projected[:], scalar=gain[:, i : i + 1], in1=target, op0=ALU.mult, op1=ALU.add
                 )
             if half == HALVES - 1:
-                nc.sync.dma_start(out=out[b, channels, :], in_=results[b, i][:])
+                finished.append((b, i))
+                if KINDS[b][i] != "C":
+                    store(b, i)
+                if len(finished) > 2 and KINDS[finished[-3][0]][finished[-3][1]] == "C":
+                    store(*finished[-3])
+
+        finished = []
+
+        def store(b, i):
+            nc.sync.dma_start(out=out[b, i * P : (i + 1) * P, :], in_=results[b, i][:])
 
         regroup_values(0, 0, "V")
         transpose_block(0)
@@ -281,13 +297,23 @@ def tile_sgcam_pb_kernel(
         for n in range(BLOCKS):
             if n in (0, 1):
                 regroup_values(1, n, "V")
+            if n == 0:
+                cast_vectors()
+            if n == 1:
+                gain_and_shift(0)
+            if n == 2:
+                gain_and_shift(4)
             if n + 1 < BLOCKS:
                 quantise_affinity(n + 1)
+            if n == 1:
+                gain_and_shift(1)
             first_product(n, "SS")
+            if n == 1:
+                gain_and_shift(2)
             if n in (0, 1):
                 quantise_values(1, n)
             if n == 1:
-                finish_gain_and_shift()
+                gain_and_shift(3)
             for k in range(SHIFTS[n]):
                 add_shift(*shifts.pop(0))
             for k in range(UNITS[n]):
@@ -295,7 +321,7 @@ def tile_sgcam_pb_kernel(
             if n + 2 < BLOCKS:
                 transpose_block(n + 2)
             if n == 0:
-                make_gain_and_shift()
+                turn_vectors()
             if n % 2:
                 quantise_y(n // QUARTERS, n % QUARTERS // 2)
         for b, i in shifts:

@@ -135,8 +135,8 @@ def tile_sgcam_pb_kernel(
             if g == 0:
                 g_grouped[b] = stage.tile([P, PASSES, INNER * LANES], BF16, name="g_grouped", bufs=1, align_bytes=64)
             copy_on[engine](
-                out=g_grouped[b][:, g, :].rearrange("j (l m i s) -> j l m s i", l=LANES, i=4, s=LANES),
-                in_=g_raw[b][:, g].rearrange("j s (m i l) -> j l m s i", i=4, l=LANES),
+                out=g_grouped[b][:, g, :].rearrange("j (l m i s) -> j m l s i", l=LANES, i=2, s=LANES),
+                in_=g_raw[b][:, g].rearrange("j s (m i l) -> j m l s i", i=2, l=LANES),
             )
 
         def quantise_values(b, g):

from contextlib import ExitStack

import concourse.mybir as mybir
from concourse.masks import make_identity

F32 = mybir.dt.float32
BF16 = mybir.dt.bfloat16
I32 = mybir.dt.int32
U32 = mybir.dt.uint32
U8 = mybir.dt.uint8
FP8X4 = mybir.dt.float8_e4m3fn_x4
ALU = mybir.AluOpType
ACT = mybir.ActivationFunctionType

P = 128
LANES = 4
K_PASS = P * LANES
BANK = 512

BATCH = 2
POINTS = 1024
INNER = 512
CHANNELS = 1024
EPS = 1e-5

PASSES = POINTS // K_PASS
QBLOCK = 2 * P
QUARTERS = POINTS // QBLOCK
BLOCKS = BATCH * QUARTERS
HALVES = POINTS // BANK
CTILES = CHANNELS // P

KINDS = (("G", "G", "G", "S", "G", "S", "G", "S"), ("G", "S", "C", "G", "S", "C", "G", "S"))

UNITS = (0, 0, 2, 2, 4, 4, 4, 0)
SHIFTS = (0, 0, 2, 2, 2, 2, 2, 2)
FLOPS = 2 * BATCH * (POINTS * POINTS * INNER + CHANNELS * INNER * POINTS)


def tile_sgcam_pb_kernel(
    tc, affinity, g_x, w_w_words, w_w_scales, w_b, bn_gamma, bn_beta, bn_mean, bn_var, x, out
):
    nc = tc.nc
    with ExitStack() as ctx:
        keep = ctx.enter_context(tc.tile_pool(name="keep", bufs=1))
        stage = ctx.enter_context(tc.tile_pool(name="stage", bufs=3))
        ctx.enter_context(tc.manual_schedule())
        psum = ctx.enter_context(tc.psum_pool(name="psum", bufs=8))

        identity = keep.tile([P, P], F32, name="identity")
        make_identity(nc, identity[:])
        vector_rows = keep.tile([P, P], BF16, name="vector_rows")
        nc.vector.memset(vector_rows[:], 0.0)
        epsilon = keep.tile([P, 1], F32, name="epsilon")
        nc.gpsimd.memset(epsilon[:], EPS)
        w_scales = keep.tile([P, CHANNELS], U8, name="w_scales", align_bytes=64)
        nc.vector.memset(w_scales[:].bitcast(I32), 0)
        for v, vector in enumerate((w_b, bn_gamma, bn_beta, bn_mean, bn_var)):
            nc.scalar.dma_start(
                out=vector_rows[CTILES * v : CTILES * (v + 1), :], in_=vector.rearrange("(i p) -> i p", p=P)
            )
        warm = keep.tile([P, 1], F32, name="warm")
        nc.vector.memset(warm[:], 0.0)
        nc.scalar.activation(out=warm[:], in_=warm[:], func=ACT.Sqrt)
        g_raw = {}
        a_raw = {}
        x_raw = {}
        w_codes = keep.tile([P, CHANNELS], U32, name="w_codes", align_bytes=64)

        def load_values(b, g):
            if g == 0:
                g_raw[b] = keep.tile([P, PASSES, LANES, INNER], BF16, name="g_raw%d" % b)
            nc.sync.dma_start(
                out=g_raw[b][:, g],
                in_=g_x[b, g * K_PASS : (g + 1) * K_PASS, :].rearrange("(j l) c -> j l c", l=LANES),
            )

        def load_affinity(n):
            b, quarter = divmod(n, QUARTERS)
            a_raw[n] = keep.tile([P, 2, POINTS], BF16, name="a_raw%d" % n)
            nc.sync.dma_start(
                out=a_raw[n][:],
                in_=affinity[b, quarter * QBLOCK : (quarter + 1) * QBLOCK, :].rearrange("(p r) s -> p r s", r=2),
            )

        def load_weight_scales(Q):
            nc.sync.dma_start(
                out=w_scales[32 * Q : 32 * Q + LANES, :].bitcast(I32),
                in_=w_w_scales[0, LANES * Q : LANES * (Q + 1), :].bitcast(I32),
            )

        def load_residual(n):
            b, quarter = divmod(n, QUARTERS)
            x_raw[n] = keep.tile([P, 2, POINTS], BF16, name="x_raw%d" % n)
            nc.sync.dma_start(
                out=x_raw[n][:],
                in_=x[b, quarter * 2 * P : (quarter + 1) * 2 * P, :].rearrange("(i p) q -> p i q", p=P),
            )

        load_values(0, 0)
        load_affinity(0)
        load_values(0, 1)
        load_affinity(1)
        load_values(1, 0)
        for Q in range(LANES):
            load_weight_scales(Q)
        load_affinity(2)
        load_values(1, 1)
        load_affinity(3)
        nc.sync.dma_start(out=w_codes[:].bitcast(I32), in_=w_w_words[0].rearrange("p n t -> p (n t)").bitcast(I32))
        load_residual(0)
        for n in range(QUARTERS, BLOCKS):
            load_affinity(n)
            load_residual(n - QUARTERS + 1)
        for n in range(QUARTERS + 1, BLOCKS):
            load_residual(n)

        vector_rows_f32 = keep.tile([P, P], F32, name="vector_rows_f32")
        per_channel = keep.tile([P, 5, CTILES], F32, name="per_channel")
        bias_c, gamma_c, beta_c, mean_c, var_c = [per_channel[:, v, :] for v in range(5)]
        gain = keep.tile([P, CTILES], F32, name="gain")
        deviation = keep.tile([P, CTILES], F32, name="deviation")
        shift = keep.tile([P, CTILES], F32, name="shift")

        g_grouped = {}
        g_quantised = {}
        a_grouped = {}
        a_quantised = {}
        y_grouped = {}
        y_quantised = {}
        results = {}
        copy_on = {"V": nc.vector.tensor_copy, "S": nc.scalar.copy}

        def regroup_values(b, g, engine):
            if g == 0:
                g_grouped[b] = stage.tile([P, PASSES, INNER * LANES], BF16, name="g_grouped", bufs=1, align_bytes=64)
            copy_on[engine](
                out=g_grouped[b][:, g, :].rearrange("j (l m i s) -> j m l s i", l=LANES, i=2, s=LANES),
                in_=g_raw[b][:, g].rearrange("j s (m i l) -> j m l s i", i=2, l=LANES),
            )

        def quantise_values(b, g):
            if g == 0:
                g_quantised[b] = (
                    keep.tile([P, PASSES * INNER], U32, name="g_codes%d" % b, align_bytes=64),
                    keep.tile([P, PASSES * INNER], U8, name="g_scales%d" % b, align_bytes=64),
                )
            columns = slice(g * INNER, (g + 1) * INNER)
            nc.vector.quantize_mx(
                out=g_quantised[b][0][:, columns].bitcast(FP8X4),
                scales=g_quantised[b][1][:, columns],
                in_=g_grouped[b][:, g, :],
            )

        def transpose_block(n, engines="SS"):
            words = a_raw[n][:].bitcast(F32)
            a_grouped[n] = stage.tile([P, PASSES, QBLOCK * LANES], BF16, name="a_grouped", align_bytes=64)
            for g in range(PASSES):
                turned = psum.tile([P, 2, 2, P], F32, name="turned", tag="bank")
                for r in range(2):
                    for u in range(2):
                        every_second = words[:, r, g * 2 * P + u : (g + 1) * 2 * P : 2]
                        nc.tensor.transpose(turned[:, r, u, :], every_second, identity[:])
                copy_on[engines[g]](
                    out=a_grouped[n][:, g, :].bitcast(F32).rearrange("j (p r u) -> j p r u", r=2, u=2),
                    in_=turned[:].rearrange("j r u p -> j p r u"),
                )

        def quantise_affinity(n):
            a_codes = stage.tile([P, PASSES * QBLOCK], U32, name="a_codes", align_bytes=64)
            a_scales = stage.tile([P, PASSES * QBLOCK], U8, name="a_scales", align_bytes=64)
            nc.vector.quantize_mx(
                out=a_codes[:].bitcast(FP8X4), scales=a_scales[:], in_=a_grouped[n][:].rearrange("j g c -> j (g c)")
            )
            a_quantised[n] = (a_codes, a_scales)

        def first_product(n, engines="SS"):
            b, quarter = divmod(n, QUARTERS)
            half, part = divmod(quarter, QUARTERS // HALVES)
            a_codes, a_scales = a_quantised[n]
            g_codes, g_scales = g_quantised[b]
            if part == 0:
                y_grouped[b, half] = stage.tile([P, BANK, LANES], BF16, name="y_grouped", align_bytes=64)
            for k in range(QBLOCK // P):
                sums = psum.tile([P, LANES, P], F32, name="sums", tag="bank")
                for l in range(LANES):
                    for g in range(PASSES):
                        stationary = slice(g * INNER + l * P, g * INNER + (l + 1) * P)
                        moving = slice(g * QBLOCK + k * P, g * QBLOCK + (k + 1) * P)
                        nc.tensor.matmul_mx(
                            out=sums[:, l, :],
                            lhsT=g_codes[:, stationary].bitcast(FP8X4),
                            lhsT_scale=g_scales[:, stationary],
                            rhs=a_codes[:, moving].bitcast(FP8X4),
                            rhs_scale=a_scales[:, moving],
                            start=(g == 0),
                            stop=(g == PASSES - 1),
                        )
                first = part * QBLOCK + k * P
                copy_on[engines[k]](
                    out=y_grouped[b, half][:, first : first + P, :], in_=sums[:].rearrange("m l q -> m q l")
                )

        def quantise_y(b, half):
            y_codes = keep.tile([P, BANK], U32, name="y_codes%d_%d" % (b, half), align_bytes=64)
            y_scales = keep.tile([P, BANK], U8, name="y_scales%d_%d" % (b, half), align_bytes=64)
            nc.vector.quantize_mx(
                out=y_codes[:].bitcast(FP8X4),
                scales=y_scales[:],
                in_=y_grouped[b, half][:].rearrange("m q l -> m (q l)"),
            )
            y_quantised[b, half] = (y_codes, y_scales)

        def cast_vectors():
            nc.vector.tensor_copy(out=vector_rows_f32[:], in_=vector_rows[:])

        def turn_vectors():
            turned_vectors = psum.tile([P, BANK], F32, name="turned_vectors", tag="bank")
            nc.tensor.transpose(turned_vectors[:, 0:P], vector_rows_f32[:], identity[:])
            nc.scalar.copy(out=per_channel[:].rearrange("p v i -> p (v i)"), in_=turned_vectors[:, 0 : 5 * CTILES])
            nc.scalar.activation(out=deviation[:], in_=var_c, func=ACT.Sqrt, bias=epsilon[:])

        def gain_and_shift(step):
            if step == 0:
                nc.vector.tensor_tensor(out=shift[:], in0=bias_c, in1=mean_c, op=ALU.subtract)
            elif step == 1:
                nc.vector.reciprocal(out=gain[:], in_=deviation[:])
            elif step == 2:
                nc.vector.tensor_tensor(out=gain[:], in0=gain[:], in1=gamma_c, op=ALU.mult)
            elif step == 3:
                nc.vector.tensor_tensor(out=shift[:], in0=shift[:], in1=gain[:], op=ALU.mult)
            else:
                nc.vector.tensor_tensor(out=shift[:], in0=shift[:], in1=beta_c, op=ALU.add)

        def add_shift(b, i):
            residual = x_raw[b * QUARTERS + i // 2][:, i % 2, :]
            if KINDS[b][i] == "C":
                return
            results[b, i] = keep.tile([P, POINTS], F32, name="result%d_%d" % (b, i))
            if KINDS[b][i] == "S":
                nc.scalar.activation(out=results[b, i][:], in_=residual, func=ACT.Identity, bias=shift[:, i : i + 1])
            else:
                nc.gpsimd.tensor_scalar(
                    out=results[b, i][:], in0=residual, scalar1=1.0, scalar2=shift[:, i : i + 1], op0=ALU.mult, op1=ALU.add
                )

        def second_product(b, half, i):
            channels = slice(i * P, (i + 1) * P)
            points = slice(half * BANK, (half + 1) * BANK)
            y_codes, y_scales = y_quantised[b, half]
            projected = psum.tile([P, BANK], F32, name="projected", tag="bank")
            nc.tensor.matmul_mx(
                out=projected[:],
                lhsT=w_codes[:, channels].bitcast(FP8X4),
                lhsT_scale=w_scales[:, channels],
                rhs=y_codes[:].bitcast(FP8X4),
                rhs_scale=y_scales[:],
                start=True,
                stop=True,
            )
            if (b, i) not in results:
                results[b, i] = keep.tile([P, POINTS], F32, name="result%d_%d" % (b, i))
            target = results[b, i][:, points]
            if KINDS[b][i] == "C":
                nc.scalar.activation(
                    out=target, in_=projected[:], func=ACT.Identity, scale=gain[:, i : i + 1], bias=shift[:, i : i + 1]
                )
                residual = x_raw[b * QUARTERS + i // 2][:, i % 2, points]
                nc.gpsimd.tensor_tensor(out=target, in0=target, in1=residual, op=ALU.add)
            else:
                nc.vector.scalar_tensor_tensor(
                    out=target, in0=projected[:], scalar=gain[:, i : i + 1], in1=target, op0=ALU.mult, op1=ALU.add
                )
            if half == HALVES - 1:
                finished.append((b, i))
                if KINDS[b][i] != "C":
                    store(b, i)
                if len(finished) > 2 and KINDS[finished[-3][0]][finished[-3][1]] == "C":
                    store(*finished[-3])

        finished = []

        def store(b, i):
            nc.sync.dma_start(out=out[b, i * P : (i + 1) * P, :], in_=results[b, i][:])

        regroup_values(0, 0, "V")
        transpose_block(0)
        quantise_values(0, 0)
        regroup_values(0, 1, "V")
        quantise_affinity(0)
        quantise_values(0, 1)
        transpose_block(1)
        units = [(0, half, i) for half in range(HALVES) for i in range(4)]
        units += [(0, half, i) for i in range(4, CTILES) for half in range(HALVES)]
        units += [(1, half, i) for i in range(CTILES) for half in range(HALVES)]
        shifts = [(b, i) for b in range(BATCH) for i in range(CTILES)]
        for n in range(BLOCKS):
            if n in (0, 1):
                regroup_values(1, n, "V")
            if n == 0:
                cast_vectors()
            if n == 1:
                gain_and_shift(0)
            if n == 2:
                gain_and_shift(4)
            if n + 1 < BLOCKS:
                quantise_affinity(n + 1)
            if n == 1:
                gain_and_shift(1)
            first_product(n, "SS")
            if n == 1:
                gain_and_shift(2)
            if n in (0, 1):
                quantise_values(1, n)
            if n == 1:
                gain_and_shift(3)
            for k in range(SHIFTS[n]):
                add_shift(*shifts.pop(0))
            for k in range(UNITS[n]):
                second_product(*units.pop(0))
            if n + 2 < BLOCKS:
                transpose_block(n + 2)
            if n == 0:
                turn_vectors()
            if n % 2:
                quantise_y(n // QUARTERS, n % QUARTERS // 2)
        for b, i in shifts:
            add_shift(b, i)
        for unit in units:
            second_product(*unit)
